import numpy as np
import ml_dtypes


def mxq(x, axis, fmt="e4m3"):
    dtype, down = {"e4m3": (ml_dtypes.float8_e4m3fn, 7), "e5m2": (ml_dtypes.float8_e5m2, 14)}[fmt]
    v = np.moveaxis(np.asarray(x, np.float32).astype(ml_dtypes.bfloat16).astype(np.float64), axis, -1)
    blocks = v.reshape(v.shape[:-1] + (-1, 32))
    amax = np.abs(blocks).max(-1, keepdims=True)
    byte = np.maximum(np.where(amax > 0, np.frexp(amax)[1] - 1 + 127, 0) - down, 1)
    scale = np.exp2(byte - 127.0)
    codes = (blocks / scale).astype(np.float32).astype(dtype).astype(np.float64)
    return np.moveaxis((codes * scale).reshape(v.shape), -1, axis)


WIDE = False


def mx_kscale(k):
    if not WIDE:
        return np.ones(k)
    levels = np.array([10, -10, 5, -5, 0])
    a = np.random.permutation(np.resize(levels, k // 512 * 4)).reshape(k // 512, 4)
    idx = np.arange(k)
    return np.exp2(a[idx // 512, idx % 128 // 32])


BF16 = ml_dtypes.bfloat16


def bf(x):
    return np.asarray(x, np.float32).astype(BF16)


def f64(x):
    return np.asarray(x).astype(np.float64)


E2M1 = np.array([0.0, 0.5, 1.0, 1.5, 2.0, 3.0, 4.0, 6.0, -0.0, -0.5, -1.0, -1.5, -2.0, -3.0, -4.0, -6.0])


def pack_weight(w, fmt):
    k, n = w.shape
    w = f64(bf(w)).reshape(k // 32, 32, n)
    amax = np.abs(w).max(1)
    if fmt == "e4m3":
        byte = np.frexp(amax)[1] - 1 + 127 - 7
    else:
        mant, ex = np.frexp(amax / 6.0)
        byte = np.where(mant > 0.5, ex, ex - 1) + 127
    byte = np.clip(np.where(amax > 0, byte, 1), 1, 254)
    scaled = (w * np.exp2(127.0 - byte)[:, None, :]).reshape(k, n).astype(np.float32)
    by_word = np.ascontiguousarray(scaled.reshape(k // 512, 128, 4, n).transpose(0, 1, 3, 2))
    if fmt == "e4m3":
        words = by_word.astype(ml_dtypes.float8_e4m3fn).view(np.uint8)
    else:
        c = by_word.astype(ml_dtypes.float4_e2m1fn).view(np.uint8) & 0xF
        words = c[..., 0::2] | (c[..., 1::2] << 4)
    return np.ascontiguousarray(words), np.ascontiguousarray(byte.astype(np.uint8).reshape(k // 512, 16, n))


def unpack_weight(words, scales, fmt):
    g, p, n, _ = words.shape
    if fmt == "e4m3":
        vals = np.ascontiguousarray(words).view(ml_dtypes.float8_e4m3fn).astype(np.float64)
    else:
        nib = np.empty((g, p, n, 4), np.uint8)
        nib[..., 0::2] = words & 0xF
        nib[..., 1::2] = words >> 4
        vals = E2M1[nib]
    vals = vals * np.repeat(np.exp2(scales.astype(np.float64) - 127.0), 8, axis=1)[..., None]
    return vals.transpose(0, 1, 3, 2).reshape(g * 512, n)


B, L, D, H, HD, FF = 2, 64, 8192, 8, 128, 4096
EPS = 1e-6
DA = H * HD


def rmsnorm(x, w):
    return x * (1.0 / np.sqrt(np.mean(x * x, axis=-1, keepdims=True) + EPS)) * w


def setup_inputs():
    s = mx_kscale(D)
    x = bf(np.random.standard_normal((B, L, D)))
    norm1_w = bf((1.0 + 0.1 * np.random.standard_normal(D)) * s)
    qkv_w = np.random.standard_normal((3 * DA, D)) / np.sqrt(D) / s[None, :]
    words, scales = pack_weight(np.ascontiguousarray(qkv_w.T), "e4m3")
    return {"x": x,
            "norm1_w": norm1_w,
            "qkv_w_words": words,
            "qkv_w_scales": scales}


def reference(x, norm1_w, qkv_w_words, qkv_w_scales):
    h = rmsnorm(f64(x), f64(norm1_w))
    qkv = mxq(h, 2, "e4m3") @ unpack_weight(qkv_w_words, qkv_w_scales, "e4m3")
    qkv = qkv.reshape(B, L, 3, H, HD)
    q, k, v = (np.moveaxis(qkv, 2, 0)[i].transpose(0, 2, 1, 3) for i in range(3))
    return q, k, v

@@ -1,0 +1,191 @@
+from contextlib import ExitStack
+
+import concourse.mybir as mybir
+from concourse.masks import make_identity
+
+F32 = mybir.dt.float32
+BF16 = mybir.dt.bfloat16
+I32 = mybir.dt.int32
+U32 = mybir.dt.uint32
+U8 = mybir.dt.uint8
+FP8X4 = mybir.dt.float8_e4m3fn_x4
+ACT = mybir.ActivationFunctionType
+ALU = mybir.AluOpType
+
+P = 128
+PACK = 4
+K_PASS = P * PACK
+BATCH = 2
+HEAD_DIM = 128
+D_MODEL = 8192
+N_OUT = 3072
+PASSES = D_MODEL // K_PASS
+BANK_COLS = 512
+BANKS = N_OUT // BANK_COLS
+BANKS_PER_OUTPUT = BANKS // 3
+HEADS_PER_BANK = BANK_COLS // HEAD_DIM
+EPS = 1e-6
+
+X_CHUNKS = 4
+X_CHUNK_COLS = D_MODEL // X_CHUNKS
+PLANES_PER_TILE = 4
+PLANE_SETS = PASSES // PLANES_PER_TILE
+QUADRANTS = 4
+PASSES_PER_QUANTISE = 4
+WEIGHT_BUFS = 12
+
+FLOPS = 2 * P * D_MODEL * N_OUT
+
+
+def tile_transformerblock_pa_k_kernel(
+    tc, x, norm1_w, qkv_w_words, qkv_w_scales, out_0, out_1, out_2
+):
+    nc = tc.nc
+    outputs = (out_0, out_1, out_2)
+
+    with ExitStack() as ctx:
+        keep = ctx.enter_context(tc.tile_pool(name="keep", bufs=1))
+        squares_pool = ctx.enter_context(tc.tile_pool(name="squares", bufs=2))
+        sorted_pool = ctx.enter_context(tc.tile_pool(name="sorted", bufs=3))
+        grouped_pool = ctx.enter_context(tc.tile_pool(name="grouped", bufs=2))
+        weight_pool = ctx.enter_context(tc.tile_pool(name="weight", bufs=WEIGHT_BUFS))
+        result_pool = ctx.enter_context(tc.tile_pool(name="result", bufs=BANKS))
+        flip_psum = ctx.enter_context(tc.psum_pool(name="flip", bufs=2))
+        acc_psum = ctx.enter_context(tc.psum_pool(name="acc", bufs=1))
+
+
+        x_sb = keep.tile([P, D_MODEL], BF16)
+        x_by_token = x.rearrange("b l d -> l b d")
+        for chunk in range(X_CHUNKS):
+            cols = slice(chunk * X_CHUNK_COLS, (chunk + 1) * X_CHUNK_COLS)
+            nc.sync.dma_start(out=x_sb[:, cols], in_=x_by_token[:, :, cols])
+
+        gain_rows = keep.tile([P, K_PASS], BF16)
+        nc.vector.memset(gain_rows[:], 0.0)
+        nc.sync.dma_start(
+            out=gain_rows[0:PASSES, :], in_=norm1_w.rearrange("(g k) -> g k", k=K_PASS)
+        )
+
+        w_planes = keep.tile([P, PLANE_SETS, N_OUT], U8, align_bytes=64)
+        nc.vector.memset(w_planes[:].bitcast(I32), 0)
+        for plane_set in range(PLANE_SETS):
+            first_pass = plane_set * PLANES_PER_TILE
+            for quadrant in range(QUADRANTS):
+                nc.sync.dma_start(
+                    out=w_planes[32 * quadrant : 32 * quadrant + 16, plane_set, :].bitcast(I32),
+                    in_=qkv_w_scales[
+                        first_pass : first_pass + PLANES_PER_TILE,
+                        4 * quadrant : 4 * quadrant + 4,
+                        :,
+                    ].bitcast(I32),
+                )
+
+        identity = keep.tile([P, P], F32)
+        make_identity(nc, identity[:])
+
+        gain_sorted = keep.tile([P, PACK, P], F32)
+        nc.vector.tensor_copy(
+            out=gain_sorted[:], in_=gain_rows[:].rearrange("g (p t) -> g t p", t=PACK)
+        )
+        gain_flipped = flip_psum.tile([P, PACK, P], F32, tag="flipped")
+        for t in range(PACK):
+            nc.tensor.transpose(gain_flipped[:, t, :], gain_sorted[:, t, :], identity[:])
+        gain_q = keep.tile([P, PASSES, PACK], F32)
+        nc.vector.tensor_copy(
+            out=gain_q[:], in_=gain_flipped[:, :, 0:PASSES].rearrange("p t g -> p g t")
+        )
+
+        chunk_sums = keep.tile([P, X_CHUNKS], F32)
+        for chunk in range(X_CHUNKS):
+            cols = slice(chunk * X_CHUNK_COLS, (chunk + 1) * X_CHUNK_COLS)
+            squares = squares_pool.tile([P, X_CHUNK_COLS], BF16)
+            nc.scalar.activation(
+                out=squares[:],
+                in_=x_sb[:, cols],
+                func=ACT.Square,
+                accum_out=chunk_sums[:, chunk : chunk + 1],
+            )
+        sum_sq = keep.tile([P, 1], F32)
+        nc.vector.reduce_sum(out=sum_sq[:], in_=chunk_sums[:], axis=mybir.AxisListType.X)
+        mean_sq = keep.tile([P, 1], F32)
+        nc.vector.tensor_scalar(
+            out=mean_sq[:],
+            in0=sum_sq[:],
+            scalar1=1.0 / D_MODEL,
+            scalar2=EPS,
+            op0=ALU.mult,
+            op1=ALU.add,
+        )
+        rms = keep.tile([P, 1], F32)
+        nc.scalar.activation(out=rms[:], in_=mean_sq[:], func=ACT.Sqrt)
+        rstd = keep.tile([P, 1], F32)
+        nc.vector.reciprocal(out=rstd[:], in_=rms[:])
+
+        h_words = keep.tile([P, PASSES, P], U32, align_bytes=64)
+        h_planes = keep.tile([P, PASSES, P], U8, align_bytes=64)
+        for first_pass in range(0, PASSES, PASSES_PER_QUANTISE):
+            grouped = grouped_pool.tile([P, PASSES_PER_QUANTISE, P, PACK], BF16, align_bytes=64)
+            for i in range(PASSES_PER_QUANTISE):
+                g = first_pass + i
+                x_sorted = sorted_pool.tile([P, PACK, P], F32)
+                nc.scalar.activation(
+                    out=x_sorted[:],
+                    in_=x_sb[:, g * K_PASS : (g + 1) * K_PASS].rearrange(
+                        "r (p t) -> r t p", t=PACK
+                    ),
+                    func=ACT.Copy,
+                    scale=rstd[:, 0:1],
+                )
+                x_flipped = flip_psum.tile([P, PACK, P], F32, tag="flipped")
+                for t in range(PACK):
+                    nc.tensor.transpose(x_flipped[:, t, :], x_sorted[:, t, :], identity[:])
+                nc.vector.tensor_tensor(
+                    out=grouped[:, i],
+                    in0=x_flipped[:].rearrange("p t r -> p r t"),
+                    in1=gain_q[:, g, :].unsqueeze(1).to_broadcast([P, P, PACK]),
+                    op=ALU.mult,
+                )
+            passes = slice(first_pass, first_pass + PASSES_PER_QUANTISE)
+            nc.vector.quantize_mx(
+                out=h_words[:, passes, :].rearrange("p g r -> p (g r)").bitcast(FP8X4),
+                scales=h_planes[:, passes, :].rearrange("p g r -> p (g r)"),
+                in_=grouped[:].rearrange("p g r t -> p (g r t)"),
+            )
+
+        acc = [
+            acc_psum.tile([P, BANK_COLS], F32, name="acc%d" % bank) for bank in range(BANKS)
+        ]
+        for g in range(PASSES):
+            w_words = weight_pool.tile([P, N_OUT], U32, align_bytes=64)
+            nc.sync.dma_start(
+                out=w_words[:].bitcast(I32),
+                in_=qkv_w_words[g].rearrange("p n t -> p (n t)").bitcast(I32),
+            )
+            plane_start = PACK * (g % PLANES_PER_TILE)
+            for bank in range(BANKS):
+                cols = slice(bank * BANK_COLS, (bank + 1) * BANK_COLS)
+                nc.tensor.matmul_mx(
+                    out=acc[bank][:],
+                    lhsT=h_words[:, g, :].bitcast(FP8X4),
+                    lhsT_scale=h_planes[:, g, :],
+                    rhs=w_words[:, cols].bitcast(FP8X4),
+                    rhs_scale=w_planes[plane_start:P, g // PLANES_PER_TILE, cols],
+                    start=(g == 0),
+                    stop=(g == PASSES - 1),
+                )
+
+        for bank in range(BANKS):
+            result = result_pool.tile([P, BANK_COLS], F32)
+            if bank % 2 == 0:
+                nc.scalar.copy(out=result[:], in_=acc[bank][:])
+            else:
+                nc.vector.tensor_copy(out=result[:], in_=acc[bank][:])
+            output = outputs[bank // BANKS_PER_OUTPUT]
+            first_head = (bank % BANKS_PER_OUTPUT) * HEADS_PER_BANK
+            for b in range(BATCH):
+                nc.sync.dma_start(
+                    out=output[b, first_head : first_head + HEADS_PER_BANK].rearrange(
+                        "h l j -> l h j"
+                    ),
+                    in_=result[b:P:BATCH, :].rearrange("l (h j) -> l h j", j=HEAD_DIM),
+                )

@@ -156,11 +156,12 @@ def tile_transformerblock_pa_k_kernel(
             acc_psum.tile([P, BANK_COLS], F32, name="acc%d" % bank) for bank in range(BANKS)
         ]
         for g in range(PASSES):
+            load_cols = BANK_COLS if g == PASSES - 1 else N_OUT
             w_words = weight_pool.tile([P, N_OUT], U32, align_bytes=64)
-            nc.sync.dma_start(
-                out=w_words[:].bitcast(I32),
-                in_=qkv_w_words[g].rearrange("p n t -> p (n t)").bitcast(I32),
-            )
+            words_in_hbm = qkv_w_words[g].rearrange("p n t -> p (n t)").bitcast(I32)
+            for first_col in range(0, N_OUT, load_cols):
+                cols = slice(first_col, first_col + load_cols)
+                nc.sync.dma_start(out=w_words[:, cols].bitcast(I32), in_=words_in_hbm[:, cols])
             plane_start = PACK * (g % PLANES_PER_TILE)
             for bank in range(BANKS):
                 cols = slice(bank * BANK_COLS, (bank + 1) * BANK_COLS)

@@ -71,13 +71,13 @@ def tile_transformerblock_pa_k_kernel(
         for plane_set in range(PLANE_SETS):
             first_pass = plane_set * PLANES_PER_TILE
             for quadrant in range(QUADRANTS):
-                nc.sync.dma_start(
-                    out=w_planes[32 * quadrant : 32 * quadrant + 16, plane_set, :].bitcast(I32),
+                nc.gpsimd.dma_start(
+                    out=w_planes[32 * quadrant : 32 * quadrant + 16, plane_set, :].bitcast(F32),
                     in_=qkv_w_scales[
                         first_pass : first_pass + PLANES_PER_TILE,
                         4 * quadrant : 4 * quadrant + 4,
                         :,
-                    ].bitcast(I32),
+                    ].bitcast(F32),
                 )
 
         identity = keep.tile([P, P], F32)

@@ -32,7 +32,7 @@ PLANES_PER_TILE = 4
 PLANE_SETS = PASSES // PLANES_PER_TILE
 QUADRANTS = 4
 PASSES_PER_QUANTISE = 4
-WEIGHT_BUFS = 12
+WEIGHT_BUFS = 13
 
 FLOPS = 2 * P * D_MODEL * N_OUT
 
@@ -60,25 +60,27 @@ def tile_transformerblock_pa_k_kernel(
             cols = slice(chunk * X_CHUNK_COLS, (chunk + 1) * X_CHUNK_COLS)
             nc.sync.dma_start(out=x_sb[:, cols], in_=x_by_token[:, :, cols])
 
-        gain_rows = keep.tile([P, K_PASS], BF16)
-        nc.vector.memset(gain_rows[:], 0.0)
-        nc.sync.dma_start(
-            out=gain_rows[0:PASSES, :], in_=norm1_w.rearrange("(g k) -> g k", k=K_PASS)
-        )
-
-        w_planes = keep.tile([P, PLANE_SETS, N_OUT], U8, align_bytes=64)
-        nc.vector.memset(w_planes[:].bitcast(I32), 0)
+        w_planes = []
         for plane_set in range(PLANE_SETS):
+            planes = keep.tile([P, N_OUT], U8, align_bytes=64, name="planes%d" % plane_set)
+            nc.vector.memset(planes[:].bitcast(I32), 0)
+            w_planes.append(planes)
             first_pass = plane_set * PLANES_PER_TILE
             for quadrant in range(QUADRANTS):
                 nc.gpsimd.dma_start(
-                    out=w_planes[32 * quadrant : 32 * quadrant + 16, plane_set, :].bitcast(F32),
+                    out=planes[32 * quadrant : 32 * quadrant + 16, :].bitcast(F32),
                     in_=qkv_w_scales[
                         first_pass : first_pass + PLANES_PER_TILE,
                         4 * quadrant : 4 * quadrant + 4,
                         :,
                     ].bitcast(F32),
                 )
+
+        gain_rows = keep.tile([P, K_PASS], BF16)
+        nc.vector.memset(gain_rows[:], 0.0)
+        nc.scalar.dma_start(
+            out=gain_rows[0:PASSES, :], in_=norm1_w.rearrange("(g k) -> g k", k=K_PASS)
+        )
 
         identity = keep.tile([P, P], F32)
         make_identity(nc, identity[:])
@@ -170,7 +172,7 @@ def tile_transformerblock_pa_k_kernel(
                     lhsT=h_words[:, g, :].bitcast(FP8X4),
                     lhsT_scale=h_planes[:, g, :],
                     rhs=w_words[:, cols].bitcast(FP8X4),
-                    rhs_scale=w_planes[plane_start:P, g // PLANES_PER_TILE, cols],
+                    rhs_scale=w_planes[g // PLANES_PER_TILE][plane_start:P, cols],
                     start=(g == 0),
                     stop=(g == PASSES - 1),
                 )

@@ -60,6 +60,12 @@ def tile_transformerblock_pa_k_kernel(
             cols = slice(chunk * X_CHUNK_COLS, (chunk + 1) * X_CHUNK_COLS)
             nc.sync.dma_start(out=x_sb[:, cols], in_=x_by_token[:, :, cols])
 
+        gain_rows = keep.tile([P, K_PASS], BF16)
+        nc.vector.memset(gain_rows[:], 0.0)
+        nc.sync.dma_start(
+            out=gain_rows[0:PASSES, :], in_=norm1_w.rearrange("(g k) -> g k", k=K_PASS)
+        )
+
         w_planes = []
         for plane_set in range(PLANE_SETS):
             planes = keep.tile([P, N_OUT], U8, align_bytes=64, name="planes%d" % plane_set)
@@ -75,12 +81,6 @@ def tile_transformerblock_pa_k_kernel(
                         :,
                     ].bitcast(F32),
                 )
-
-        gain_rows = keep.tile([P, K_PASS], BF16)
-        nc.vector.memset(gain_rows[:], 0.0)
-        nc.scalar.dma_start(
-            out=gain_rows[0:PASSES, :], in_=norm1_w.rearrange("(g k) -> g k", k=K_PASS)
-        )
 
         identity = keep.tile([P, P], F32)
         make_identity(nc, identity[:])
@@ -101,12 +101,21 @@ def tile_transformerblock_pa_k_kernel(
         for chunk in range(X_CHUNKS):
             cols = slice(chunk * X_CHUNK_COLS, (chunk + 1) * X_CHUNK_COLS)
             squares = squares_pool.tile([P, X_CHUNK_COLS], BF16)
-            nc.scalar.activation(
-                out=squares[:],
-                in_=x_sb[:, cols],
-                func=ACT.Square,
-                accum_out=chunk_sums[:, chunk : chunk + 1],
-            )
+            chunk_sum = chunk_sums[:, chunk : chunk + 1]
+            if chunk % 2 == 0:
+                nc.scalar.activation(
+                    out=squares[:], in_=x_sb[:, cols], func=ACT.Square, accum_out=chunk_sum
+                )
+            else:
+                nc.vector.scalar_tensor_tensor(
+                    out=squares[:],
+                    in0=x_sb[:, cols],
+                    scalar=1.0,
+                    in1=x_sb[:, cols],
+                    op0=ALU.mult,
+                    op1=ALU.mult,
+                    accum_out=chunk_sum,
+                )
         sum_sq = keep.tile([P, 1], F32)
         nc.vector.reduce_sum(out=sum_sq[:], in_=chunk_sums[:], axis=mybir.AxisListType.X)
         mean_sq = keep.tile([P, 1], F32)

@@ -23,6 +23,8 @@ PASSES = D_MODEL // K_PASS
 BANK_COLS = 512
 BANKS = N_OUT // BANK_COLS
 BANKS_PER_OUTPUT = BANKS // 3
+V_BANK = 2 * BANKS_PER_OUTPUT
+STORES = [(0, 2), (2, 2), (4, 1), (5, 1)]
 HEADS_PER_BANK = BANK_COLS // HEAD_DIM
 EPS = 1e-6
 
@@ -49,7 +51,7 @@ def tile_transformerblock_pa_k_kernel(
         sorted_pool = ctx.enter_context(tc.tile_pool(name="sorted", bufs=3))
         grouped_pool = ctx.enter_context(tc.tile_pool(name="grouped", bufs=2))
         weight_pool = ctx.enter_context(tc.tile_pool(name="weight", bufs=WEIGHT_BUFS))
-        result_pool = ctx.enter_context(tc.tile_pool(name="result", bufs=BANKS))
+        result_pool = ctx.enter_context(tc.tile_pool(name="result", bufs=1))
         flip_psum = ctx.enter_context(tc.psum_pool(name="flip", bufs=2))
         acc_psum = ctx.enter_context(tc.psum_pool(name="acc", bufs=1))
 
@@ -166,38 +168,49 @@ def tile_transformerblock_pa_k_kernel(
         acc = [
             acc_psum.tile([P, BANK_COLS], F32, name="acc%d" % bank) for bank in range(BANKS)
         ]
-        for g in range(PASSES):
-            load_cols = BANK_COLS if g == PASSES - 1 else N_OUT
-            w_words = weight_pool.tile([P, N_OUT], U32, align_bytes=64)
+        last, before = PASSES - 1, PASSES - 2
+        loads = [(g, 0, BANKS) for g in range(before)]
+        loads += [(before, 0, V_BANK)] + [(last, bank, 1) for bank in range(V_BANK)]
+        loads += [(before, V_BANK, BANKS_PER_OUTPUT)]
+        loads += [(last, bank, 1) for bank in range(V_BANK, BANKS)]
+        for g, first_bank, banks in loads:
+            w_words = weight_pool.tile([P, banks * BANK_COLS], U32, align_bytes=64, name="w_words")
             words_in_hbm = qkv_w_words[g].rearrange("p n t -> p (n t)").bitcast(I32)
-            for first_col in range(0, N_OUT, load_cols):
-                cols = slice(first_col, first_col + load_cols)
-                nc.sync.dma_start(out=w_words[:, cols].bitcast(I32), in_=words_in_hbm[:, cols])
+            first_col = first_bank * BANK_COLS
+            nc.sync.dma_start(
+                out=w_words[:].bitcast(I32),
+                in_=words_in_hbm[:, first_col : first_col + banks * BANK_COLS],
+            )
             plane_start = PACK * (g % PLANES_PER_TILE)
-            for bank in range(BANKS):
+            for i in range(banks):
+                bank = first_bank + i
                 cols = slice(bank * BANK_COLS, (bank + 1) * BANK_COLS)
                 nc.tensor.matmul_mx(
                     out=acc[bank][:],
                     lhsT=h_words[:, g, :].bitcast(FP8X4),
                     lhsT_scale=h_planes[:, g, :],
-                    rhs=w_words[:, cols].bitcast(FP8X4),
+                    rhs=w_words[:, i * BANK_COLS : (i + 1) * BANK_COLS].bitcast(FP8X4),
                     rhs_scale=w_planes[g // PLANES_PER_TILE][plane_start:P, cols],
                     start=(g == 0),
-                    stop=(g == PASSES - 1),
+                    stop=(g == last),
                 )
 
-        for bank in range(BANKS):
-            result = result_pool.tile([P, BANK_COLS], F32)
-            if bank % 2 == 0:
-                nc.scalar.copy(out=result[:], in_=acc[bank][:])
-            else:
-                nc.vector.tensor_copy(out=result[:], in_=acc[bank][:])
-            output = outputs[bank // BANKS_PER_OUTPUT]
-            first_head = (bank % BANKS_PER_OUTPUT) * HEADS_PER_BANK
+        for first_bank, banks in STORES:
+            result = result_pool.tile(
+                [P, banks * BANK_COLS], F32, name="result%d" % first_bank
+            )
+            for i in range(banks):
+                bank = first_bank + i
+                cols = slice(i * BANK_COLS, (i + 1) * BANK_COLS)
+                if bank % 2 == 0:
+                    nc.scalar.copy(out=result[:, cols], in_=acc[bank][:])
+                else:
+                    nc.vector.tensor_copy(out=result[:, cols], in_=acc[bank][:])
+            output = outputs[first_bank // BANKS_PER_OUTPUT]
+            first_head = (first_bank % BANKS_PER_OUTPUT) * HEADS_PER_BANK
+            heads = banks * HEADS_PER_BANK
             for b in range(BATCH):
                 nc.sync.dma_start(
-                    out=output[b, first_head : first_head + HEADS_PER_BANK].rearrange(
-                        "h l j -> l h j"
-                    ),
+                    out=output[b, first_head : first_head + heads].rearrange("h l j -> l h j"),
                     in_=result[b:P:BATCH, :].rearrange("l (h j) -> l h j", j=HEAD_DIM),
                 )

@@ -28,12 +28,15 @@ STORES = [(0, 2), (2, 2), (4, 1), (5, 1)]
 HEADS_PER_BANK = BANK_COLS // HEAD_DIM
 EPS = 1e-6
 
+X_LOADS = 2
+X_LOAD_COLS = D_MODEL // X_LOADS
 X_CHUNKS = 4
 X_CHUNK_COLS = D_MODEL // X_CHUNKS
 PLANES_PER_TILE = 4
 PLANE_SETS = PASSES // PLANES_PER_TILE
 QUADRANTS = 4
 PASSES_PER_QUANTISE = 4
+SPLIT_PASSES = 4
 WEIGHT_BUFS = 13
 
 FLOPS = 2 * P * D_MODEL * N_OUT
@@ -58,8 +61,8 @@ def tile_transformerblock_pa_k_kernel(
 
         x_sb = keep.tile([P, D_MODEL], BF16)
         x_by_token = x.rearrange("b l d -> l b d")
-        for chunk in range(X_CHUNKS):
-            cols = slice(chunk * X_CHUNK_COLS, (chunk + 1) * X_CHUNK_COLS)
+        for load in range(X_LOADS):
+            cols = slice(load * X_LOAD_COLS, (load + 1) * X_LOAD_COLS)
             nc.sync.dma_start(out=x_sb[:, cols], in_=x_by_token[:, :, cols])
 
         gain_rows = keep.tile([P, K_PASS], BF16)
@@ -168,10 +171,11 @@ def tile_transformerblock_pa_k_kernel(
         acc = [
             acc_psum.tile([P, BANK_COLS], F32, name="acc%d" % bank) for bank in range(BANKS)
         ]
-        last, before = PASSES - 1, PASSES - 2
-        loads = [(g, 0, BANKS) for g in range(before)]
-        loads += [(before, 0, V_BANK)] + [(last, bank, 1) for bank in range(V_BANK)]
-        loads += [(before, V_BANK, BANKS_PER_OUTPUT)]
+        last = PASSES - 1
+        split = range(PASSES - SPLIT_PASSES, PASSES)
+        loads = [(g, 0, BANKS) for g in range(split.start)]
+        loads += [(g, 0, V_BANK) for g in split]
+        loads += [(g, V_BANK, BANKS_PER_OUTPUT) for g in split if g != last]
         loads += [(last, bank, 1) for bank in range(V_BANK, BANKS)]
         for g, first_bank, banks in loads:
             w_words = weight_pool.tile([P, banks * BANK_COLS], U32, align_bytes=64, name="w_words")

from contextlib import ExitStack

import concourse.mybir as mybir
from concourse.masks import make_identity

F32 = mybir.dt.float32
BF16 = mybir.dt.bfloat16
I32 = mybir.dt.int32
U32 = mybir.dt.uint32
U8 = mybir.dt.uint8
FP8X4 = mybir.dt.float8_e4m3fn_x4
ACT = mybir.ActivationFunctionType
ALU = mybir.AluOpType

P = 128
PACK = 4
K_PASS = P * PACK
BATCH = 2
HEAD_DIM = 128
D_MODEL = 8192
N_OUT = 3072
PASSES = D_MODEL // K_PASS
BANK_COLS = 512
BANKS = N_OUT // BANK_COLS
BANKS_PER_OUTPUT = BANKS // 3
V_BANK = 2 * BANKS_PER_OUTPUT
STORES = [(0, 2), (2, 2), (4, 1), (5, 1)]
HEADS_PER_BANK = BANK_COLS // HEAD_DIM
EPS = 1e-6

X_LOADS = 2
X_LOAD_COLS = D_MODEL // X_LOADS
X_CHUNKS = 4
X_CHUNK_COLS = D_MODEL // X_CHUNKS
PLANES_PER_TILE = 4
PLANE_SETS = PASSES // PLANES_PER_TILE
QUADRANTS = 4
PASSES_PER_QUANTISE = 4
SPLIT_PASSES = 4
WEIGHT_BUFS = 13

FLOPS = 2 * P * D_MODEL * N_OUT


def tile_transformerblock_pa_k_kernel(
    tc, x, norm1_w, qkv_w_words, qkv_w_scales, out_0, out_1, out_2
):
    nc = tc.nc
    outputs = (out_0, out_1, out_2)

    with ExitStack() as ctx:
        keep = ctx.enter_context(tc.tile_pool(name="keep", bufs=1))
        squares_pool = ctx.enter_context(tc.tile_pool(name="squares", bufs=2))
        sorted_pool = ctx.enter_context(tc.tile_pool(name="sorted", bufs=3))
        grouped_pool = ctx.enter_context(tc.tile_pool(name="grouped", bufs=2))
        weight_pool = ctx.enter_context(tc.tile_pool(name="weight", bufs=WEIGHT_BUFS))
        result_pool = ctx.enter_context(tc.tile_pool(name="result", bufs=1))
        flip_psum = ctx.enter_context(tc.psum_pool(name="flip", bufs=2))
        acc_psum = ctx.enter_context(tc.psum_pool(name="acc", bufs=1))


        x_sb = keep.tile([P, D_MODEL], BF16)
        x_by_token = x.rearrange("b l d -> l b d")
        for load in range(X_LOADS):
            cols = slice(load * X_LOAD_COLS, (load + 1) * X_LOAD_COLS)
            nc.sync.dma_start(out=x_sb[:, cols], in_=x_by_token[:, :, cols])

        gain_rows = keep.tile([P, K_PASS], BF16)
        nc.vector.memset(gain_rows[:], 0.0)
        nc.sync.dma_start(
            out=gain_rows[0:PASSES, :], in_=norm1_w.rearrange("(g k) -> g k", k=K_PASS)
        )

        w_planes = []
        for plane_set in range(PLANE_SETS):
            planes = keep.tile([P, N_OUT], U8, align_bytes=64, name="planes%d" % plane_set)
            nc.vector.memset(planes[:].bitcast(I32), 0)
            w_planes.append(planes)
            first_pass = plane_set * PLANES_PER_TILE
            for quadrant in range(QUADRANTS):
                nc.gpsimd.dma_start(
                    out=planes[32 * quadrant : 32 * quadrant + 16, :].bitcast(F32),
                    in_=qkv_w_scales[
                        first_pass : first_pass + PLANES_PER_TILE,
                        4 * quadrant : 4 * quadrant + 4,
                        :,
                    ].bitcast(F32),
                )

        identity = keep.tile([P, P], F32)
        make_identity(nc, identity[:])

        gain_sorted = keep.tile([P, PACK, P], F32)
        nc.vector.tensor_copy(
            out=gain_sorted[:], in_=gain_rows[:].rearrange("g (p t) -> g t p", t=PACK)
        )
        gain_flipped = flip_psum.tile([P, PACK, P], F32, tag="flipped")
        for t in range(PACK):
            nc.tensor.transpose(gain_flipped[:, t, :], gain_sorted[:, t, :], identity[:])
        gain_q = keep.tile([P, PASSES, PACK], F32)
        nc.vector.tensor_copy(
            out=gain_q[:], in_=gain_flipped[:, :, 0:PASSES].rearrange("p t g -> p g t")
        )

        chunk_sums = keep.tile([P, X_CHUNKS], F32)
        for chunk in range(X_CHUNKS):
            cols = slice(chunk * X_CHUNK_COLS, (chunk + 1) * X_CHUNK_COLS)
            squares = squares_pool.tile([P, X_CHUNK_COLS], BF16)
            chunk_sum = chunk_sums[:, chunk : chunk + 1]
            if chunk % 2 == 0:
                nc.scalar.activation(
                    out=squares[:], in_=x_sb[:, cols], func=ACT.Square, accum_out=chunk_sum
                )
            else:
                nc.vector.scalar_tensor_tensor(
                    out=squares[:],
                    in0=x_sb[:, cols],
                    scalar=1.0,
                    in1=x_sb[:, cols],
                    op0=ALU.mult,
                    op1=ALU.mult,
                    accum_out=chunk_sum,
                )
        sum_sq = keep.tile([P, 1], F32)
        nc.vector.reduce_sum(out=sum_sq[:], in_=chunk_sums[:], axis=mybir.AxisListType.X)
        mean_sq = keep.tile([P, 1], F32)
        nc.vector.tensor_scalar(
            out=mean_sq[:],
            in0=sum_sq[:],
            scalar1=1.0 / D_MODEL,
            scalar2=EPS,
            op0=ALU.mult,
            op1=ALU.add,
        )
        rms = keep.tile([P, 1], F32)
        nc.scalar.activation(out=rms[:], in_=mean_sq[:], func=ACT.Sqrt)
        rstd = keep.tile([P, 1], F32)
        nc.vector.reciprocal(out=rstd[:], in_=rms[:])

        h_words = keep.tile([P, PASSES, P], U32, align_bytes=64)
        h_planes = keep.tile([P, PASSES, P], U8, align_bytes=64)
        for first_pass in range(0, PASSES, PASSES_PER_QUANTISE):
            grouped = grouped_pool.tile([P, PASSES_PER_QUANTISE, P, PACK], BF16, align_bytes=64)
            for i in range(PASSES_PER_QUANTISE):
                g = first_pass + i
                x_sorted = sorted_pool.tile([P, PACK, P], F32)
                nc.scalar.activation(
                    out=x_sorted[:],
                    in_=x_sb[:, g * K_PASS : (g + 1) * K_PASS].rearrange(
                        "r (p t) -> r t p", t=PACK
                    ),
                    func=ACT.Copy,
                    scale=rstd[:, 0:1],
                )
                x_flipped = flip_psum.tile([P, PACK, P], F32, tag="flipped")
                for t in range(PACK):
                    nc.tensor.transpose(x_flipped[:, t, :], x_sorted[:, t, :], identity[:])
                nc.vector.tensor_tensor(
                    out=grouped[:, i],
                    in0=x_flipped[:].rearrange("p t r -> p r t"),
                    in1=gain_q[:, g, :].unsqueeze(1).to_broadcast([P, P, PACK]),
                    op=ALU.mult,
                )
            passes = slice(first_pass, first_pass + PASSES_PER_QUANTISE)
            nc.vector.quantize_mx(
                out=h_words[:, passes, :].rearrange("p g r -> p (g r)").bitcast(FP8X4),
                scales=h_planes[:, passes, :].rearrange("p g r -> p (g r)"),
                in_=grouped[:].rearrange("p g r t -> p (g r t)"),
            )

        acc = [
            acc_psum.tile([P, BANK_COLS], F32, name="acc%d" % bank) for bank in range(BANKS)
        ]
        last = PASSES - 1
        split = range(PASSES - SPLIT_PASSES, PASSES)
        loads = [(g, 0, BANKS) for g in range(split.start)]
        loads += [(g, 0, V_BANK) for g in split]
        loads += [(g, V_BANK, BANKS_PER_OUTPUT) for g in split if g != last]
        loads += [(last, bank, 1) for bank in range(V_BANK, BANKS)]
        for g, first_bank, banks in loads:
            w_words = weight_pool.tile([P, banks * BANK_COLS], U32, align_bytes=64, name="w_words")
            words_in_hbm = qkv_w_words[g].rearrange("p n t -> p (n t)").bitcast(I32)
            first_col = first_bank * BANK_COLS
            nc.sync.dma_start(
                out=w_words[:].bitcast(I32),
                in_=words_in_hbm[:, first_col : first_col + banks * BANK_COLS],
            )
            plane_start = PACK * (g % PLANES_PER_TILE)
            for i in range(banks):
                bank = first_bank + i
                cols = slice(bank * BANK_COLS, (bank + 1) * BANK_COLS)
                nc.tensor.matmul_mx(
                    out=acc[bank][:],
                    lhsT=h_words[:, g, :].bitcast(FP8X4),
                    lhsT_scale=h_planes[:, g, :],
                    rhs=w_words[:, i * BANK_COLS : (i + 1) * BANK_COLS].bitcast(FP8X4),
                    rhs_scale=w_planes[g // PLANES_PER_TILE][plane_start:P, cols],
                    start=(g == 0),
                    stop=(g == last),
                )

        for first_bank, banks in STORES:
            result = result_pool.tile(
                [P, banks * BANK_COLS], F32, name="result%d" % first_bank
            )
            for i in range(banks):
                bank = first_bank + i
                cols = slice(i * BANK_COLS, (i + 1) * BANK_COLS)
                if bank % 2 == 0:
                    nc.scalar.copy(out=result[:, cols], in_=acc[bank][:])
                else:
                    nc.vector.tensor_copy(out=result[:, cols], in_=acc[bank][:])
            output = outputs[first_bank // BANKS_PER_OUTPUT]
            first_head = (first_bank % BANKS_PER_OUTPUT) * HEADS_PER_BANK
            heads = banks * HEADS_PER_BANK
            for b in range(BATCH):
                nc.sync.dma_start(
                    out=output[b, first_head : first_head + heads].rearrange("h l j -> l h j"),
                    in_=result[b:P:BATCH, :].rearrange("l (h j) -> l h j", j=HEAD_DIM),
                )
